import numpy as np
import ml_dtypes


def mxq(x, axis, fmt="e4m3"):
    dtype, down = {"e4m3": (ml_dtypes.float8_e4m3fn, 7), "e5m2": (ml_dtypes.float8_e5m2, 14)}[fmt]
    v = np.moveaxis(np.asarray(x, np.float32).astype(ml_dtypes.bfloat16).astype(np.float64), axis, -1)
    blocks = v.reshape(v.shape[:-1] + (-1, 32))
    amax = np.abs(blocks).max(-1, keepdims=True)
    byte = np.maximum(np.where(amax > 0, np.frexp(amax)[1] - 1 + 127, 0) - down, 1)
    scale = np.exp2(byte - 127.0)
    codes = (blocks / scale).astype(np.float32).astype(dtype).astype(np.float64)
    return np.moveaxis((codes * scale).reshape(v.shape), -1, axis)


WIDE = False


def mx_kscale(k):
    if not WIDE:
        return np.ones(k)
    levels = np.array([10, -10, 5, -5, 0])
    if k % 512:
        return np.exp2(np.random.permutation(np.resize(levels, k // 32))).repeat(32)
    a = np.empty((k // 512, 16))
    for p in range(k // 512):
        a[p, :8] = np.random.permutation(np.resize(levels, 8))
        for g in range(8):
            far = levels[np.abs(levels - a[p, g]) >= 10]
            a[p, g + 8] = far[np.random.randint(len(far))]
    return np.exp2(a.ravel()).repeat(32)


BF16 = ml_dtypes.bfloat16


def bf(x):
    return np.asarray(x, np.float32).astype(BF16)


def f64(x):
    return np.asarray(x).astype(np.float64)


E2M1 = np.array([0.0, 0.5, 1.0, 1.5, 2.0, 3.0, 4.0, 6.0, -0.0, -0.5, -1.0, -1.5, -2.0, -3.0, -4.0, -6.0])


def pack_weight(w, fmt):
    k, n = w.shape
    w = f64(bf(w)).reshape(k // 32, 32, n)
    amax = np.abs(w).max(1)
    if fmt == "e4m3":
        byte = np.frexp(amax)[1] - 1 + 127 - 7
    else:
        mant, ex = np.frexp(amax / 6.0)
        byte = np.where(mant > 0.5, ex, ex - 1) + 127
    byte = np.clip(np.where(amax > 0, byte, 1), 1, 254)
    scaled = (w * np.exp2(127.0 - byte)[:, None, :]).reshape(k, n).astype(np.float32)
    by_word = np.ascontiguousarray(scaled.reshape(k // 512, 128, 4, n).transpose(0, 1, 3, 2))
    if fmt == "e4m3":
        words = by_word.astype(ml_dtypes.float8_e4m3fn).view(np.uint8)
    else:
        c = by_word.astype(ml_dtypes.float4_e2m1fn).view(np.uint8) & 0xF
        words = c[..., 0::2] | (c[..., 1::2] << 4)
    return np.ascontiguousarray(words), np.ascontiguousarray(byte.astype(np.uint8).reshape(k // 512, 16, n))


def unpack_weight(words, scales, fmt):
    g, p, n, _ = words.shape
    if fmt == "e4m3":
        vals = np.ascontiguousarray(words).view(ml_dtypes.float8_e4m3fn).astype(np.float64)
    else:
        nib = np.empty((g, p, n, 4), np.uint8)
        nib[..., 0::2] = words & 0xF
        nib[..., 1::2] = words >> 4
        vals = E2M1[nib]
    vals = vals * np.repeat(np.exp2(scales.astype(np.float64) - 127.0), 8, axis=1)[..., None]
    return vals.transpose(0, 1, 3, 2).reshape(g * 512, n)
def pack4(w):
    words, scales = pack_weight(w, "e2m1")
    return words.reshape(words.shape[0], 128, -1), scales


def unpack4(words, scales):
    return unpack_weight(words.reshape(words.shape[0], 128, -1, 2), scales, "e2m1")


B, S, V, E, M = 512, 16, 4096, 512, 1024


def draw0():
    s, t = mx_kscale(E), mx_kscale(M)
    y2 = bf(np.maximum(np.random.standard_normal((B, E)), 0.0) * s)
    first = bf(np.random.standard_normal((B, M)) * 0.4 * t)
    w_second = np.random.standard_normal((M, E)) * 1.4 / np.sqrt(E) / s[None, :]
    w_second_words, w_second_scales = pack4(w_second.T)
    b_second = bf(np.random.standard_normal(M) * 0.3)
    w_int = np.random.standard_normal((M, E)) * 1.4 / np.sqrt(E) / s[None, :] * t[:, None]
    w_int_words, w_int_scales = pack4(w_int.T)
    b_int = bf(np.random.standard_normal(M) * 0.3 * t)
    w_out = np.random.standard_normal((V, M)) / np.sqrt(M) / t[None, :]
    w_out_words, w_out_scales = pack4(w_out.T)
    b_out = bf(np.random.standard_normal(V) * 0.3)
    return {"y2": y2,
            "first": first,
            "w_second_words": w_second_words,
            "w_second_scales": w_second_scales,
            "b_second": b_second,
            "w_int_words": w_int_words,
            "w_int_scales": w_int_scales,
            "b_int": b_int,
            "w_out_words": w_out_words,
            "w_out_scales": w_out_scales,
            "b_out": b_out}


def core(y2, first, w_second_words, w_second_scales, b_second, w_int_words, w_int_scales, b_int, w_out_words, w_out_scales, b_out):
    y2q = mxq(f64(y2), 1, "e4m3")
    second = np.maximum((y2q @ unpack4(w_second_words, w_second_scales)) + f64(b_second), 0.0)
    inter = np.maximum((y2q @ unpack4(w_int_words, w_int_scales)) + f64(b_int), 0.0)
    z = second * f64(first) + inter
    return (mxq(z, 1, "e4m3") @ unpack4(w_out_words, w_out_scales)) + f64(b_out)


def e4m3fn_bytes(y):
    return np.clip(np.asarray(y, np.float64), -448.0, 448.0).astype(np.float32).astype(ml_dtypes.float8_e4m3fn).view(np.uint8)


def e4m3fn_values(b):
    return np.asarray(b, np.uint8).view(ml_dtypes.float8_e4m3fn).astype(np.float64)


def setup_inputs():
    d = draw0()
    x0 = np.asarray(d['y2']).astype(np.float64)
    s = (np.max(np.abs(x0), axis=(0,), keepdims=True) / 448.0).astype(np.float32)
    out = {}
    for k, v in d.items():
        if k == 'y2':
            out['y2_bytes'] = e4m3fn_bytes(x0 / s.astype(np.float64))
            out['y2_scale'] = s
        else:
            out[k] = v
    return out


def reference(y2_bytes, y2_scale, first, w_second_words, w_second_scales, b_second, w_int_words, w_int_scales, b_int, w_out_words, w_out_scales, b_out):
    return core(e4m3fn_values(y2_bytes) * y2_scale.astype(np.float64), first, w_second_words, w_second_scales, b_second, w_int_words, w_int_scales, b_int, w_out_words, w_out_scales, b_out)

@@ -1,0 +1,283 @@
+from contextlib import ExitStack
+
+import concourse.mybir as mybir
+from concourse.masks import make_identity
+
+F32 = mybir.dt.float32
+BF16 = mybir.dt.bfloat16
+I32 = mybir.dt.int32
+U32 = mybir.dt.uint32
+U8 = mybir.dt.uint8
+FP8 = mybir.dt.float8_e4m3fn
+FP8X4 = mybir.dt.float8_e4m3fn_x4
+FP4X4 = mybir.dt.float4_e2m1fn_x4
+ADD = mybir.AluOpType.add
+MULT = mybir.AluOpType.mult
+RELU = mybir.ActivationFunctionType.Relu
+
+P = 128
+ROWS, E, M, V = 512, 512, 1024, 4096
+T = 4
+TOK = 128
+TILES = ROWS // TOK
+G = M // 512
+NB = 512
+BANKS = V // NB
+
+FLOPS = 2 * ROWS * E * M * 2 + 2 * ROWS * M * V
+
+
+def tile_smcrossbaby_1_pb_w4_kernel(tc, y2_bytes, y2_scale, first, w_second_words, w_second_scales, b_second, w_int_words, w_int_scales, b_int, w_out_words, w_out_scales, b_out, out):
+    nc = tc.nc
+    with ExitStack() as ctx:
+        keep = ctx.enter_context(tc.tile_pool(name="keep", bufs=1))
+        work = ctx.enter_context(tc.tile_pool(name="work", bufs=4))
+        psum = ctx.enter_context(tc.psum_pool(name="psum", bufs=1))
+        ctx.enter_context(tc.manual_schedule())
+
+        def sb(name, width, dtype):
+            return keep.tile([P, width], dtype, name=name, align_bytes=64)
+
+        ident = sb("ident", P, F32)
+        ident16 = sb("ident16", P, BF16)
+        dummy = sb("dummy", 2, F32)
+        b_rows = sb("b_rows", NB, BF16)
+        b_all = sb("b_all", V, BF16)
+        y_bytes = sb("y_bytes", TILES * E, U8)
+        y_wide = sb("y_wide", TILES * E, BF16)
+        y_scale = sb("y_scale", T, F32)
+        y_mid = sb("y_mid", TILES * E, BF16)
+        y_codes = sb("y_codes", ROWS, U32)
+        y_planes = sb("y_planes", ROWS, U8)
+        f_rows = [sb(f"f_rows{i}", M, BF16) for i in range(TILES)]
+        w_raw = [sb(f"w_raw{w}", 2 * M, U8) for w in range(2)]
+        w_raw_sc = [sb(f"w_raw_sc{w}", M, U8) for w in range(2)]
+        w_perm = [sb(f"w_perm{w}", 2 * M, U8) for w in range(2)]
+        w_perm_sc = [sb(f"w_perm_sc{w}", M, U8) for w in range(2)]
+        bias16 = [sb(f"bias16_{w}", G * T, BF16) for w in range(2)]
+        bias = [sb(f"bias_{w}", G * T, F32) for w in range(2)]
+        wo = sb("wo", G * 2 * V, U8)
+        wo_sc = sb("wo_sc", G * V, U8)
+        z_mid = [sb(f"z_mid{i}", G * TOK * T, BF16) for i in range(TILES)]
+        z_codes = [sb(f"z_codes{i}", G * TOK, U32) for i in range(TILES)]
+        z_planes = [sb(f"z_planes{i}", G * TOK, U8) for i in range(TILES)]
+        o_tiles = [sb(f"o{i}", V, F32) for i in range(TILES)]
+
+        nc.vector.memset(dummy[:], 0.0)
+        nc.vector.memset(b_rows[:], 0.0)
+        nc.vector.memset(w_raw_sc[0][:].bitcast(I32), 0)
+        nc.vector.memset(w_raw_sc[1][:].bitcast(I32), 0)
+        nc.scalar.activation(out=dummy[:, 1:2], in_=dummy[:, 0:1], func=RELU)
+
+        yb = y2_bytes.rearrange("(i p) k -> p i k", p=P)
+        nc.sync.dma_start(out=y_bytes[:, 0:E], in_=y2_bytes[0:P, :])
+        nc.scalar.dma_start(out=y_scale[:], in_=y2_scale.rearrange("o (p t) -> p (o t)", t=T))
+        words = (w_second_words, w_int_words)
+        scales = (w_second_scales, w_int_scales)
+
+        def load_w(w):
+            nc.sync.dma_start(out=w_raw[w][:].bitcast(I32), in_=words[w][0].bitcast(I32))
+            for r in range(4):
+                nc.sync.dma_start(out=w_raw_sc[w][r:P:32, :].bitcast(I32), in_=scales[w][0][r:16:4, :].bitcast(I32))
+
+        load_w(0)
+        nc.sync.dma_start(out=y_bytes[:, E:].rearrange("p (i k) -> p i k", k=E), in_=yb[:, 1:, :])
+        load_w(1)
+        nc.gpsimd.dma_start(out=bias16[0][:].rearrange("p (g t) -> p g t", g=G), in_=b_second.rearrange("(g p t) -> p g t", p=P, t=T))
+        make_identity(nc, ident[:])
+        nc.gpsimd.dma_start(out=b_rows[0:BANKS, :], in_=b_out.rearrange("(j n) -> j n", j=BANKS))
+        nc.gpsimd.dma_start(out=bias16[1][:].rearrange("p (g t) -> p g t", g=G), in_=b_int.rearrange("(g p t) -> p g t", p=P, t=T))
+        nc.gpsimd.memset(wo_sc[:].bitcast(I32), 0)
+
+        def load_first(i):
+            nc.sync.dma_start(out=f_rows[i][:], in_=first[i * TOK:(i + 1) * TOK, :])
+
+        load_first(0)
+        load_first(1)
+        src_sc = w_out_scales.bitcast(I32).rearrange("g (q r) n -> r q g n", r=4)
+        for r in range(4):
+            nc.sync.dma_start(out=wo_sc[r:P:32, :].bitcast(I32).rearrange("p (g n) -> p g n", g=G), in_=src_sc[r])
+        src_wo = w_out_words.bitcast(I32).rearrange("g p n -> p g n")
+        dst_wo = wo[:].bitcast(I32).rearrange("p (g n) -> p g n", g=G)
+        for c in range(4):
+            nc.sync.dma_start(out=dst_wo[:, :, c * 512:(c + 1) * 512], in_=src_wo[:, :, c * 512:(c + 1) * 512])
+            if c < 2:
+                load_first(2 + c)
+
+        nc.scalar.copy(out=ident16[:], in_=ident[:])
+        for w in range(2):
+            nc.gpsimd.tensor_copy(out=bias[w][:], in_=bias16[w][:])
+
+        def widen(i, n=1):
+            nc.scalar.copy(out=y_wide[:, i * E:(i + n) * E], in_=y_bytes[:, i * E:(i + n) * E].bitcast(FP8))
+
+        def bank(name, shape, dtype):
+            return psum.tile(shape, dtype, name=name, tag="wide", bufs=4)
+
+        def spread_bias(h):
+            ps = bank("b_ps", [P, 2 * NB], BF16)
+            for e in range(2):
+                j = 2 * h + e
+                nc.tensor.matmul(ps[:, e * NB:(e + 1) * NB], lhsT=ident16[:, j:j + 1].to_broadcast([P, P]), rhs=b_rows[:], start=True, stop=True)
+            return ps
+
+        def copy_bias(h, ps):
+            nc.scalar.copy(out=b_all[:, h * 2 * NB:(h + 1) * 2 * NB], in_=ps[:])
+
+        def turn_y(i):
+            ps = bank("y_ps", [P, 2 * TOK], F32)
+            src = y_wide[:, i * E:(i + 1) * E].bitcast(F32)
+            for u in range(2):
+                nc.tensor.transpose(ps[:, u * TOK:(u + 1) * TOK], src[:, u:2 * P:2], ident[:])
+            return ps
+
+        def scale_y(i, ps):
+            nc.vector.tensor_tensor(
+                out=y_mid[:, i * E:(i + 1) * E].rearrange("p (r u e) -> p r u e", u=2, e=2),
+                in0=ps[:].bitcast(BF16).rearrange("p (u r e) -> p r u e", u=2, e=2),
+                in1=y_scale[:].rearrange("p (u e) -> p u e", e=2).unsqueeze(1).to_broadcast([P, TOK, 2, 2]),
+                op=MULT)
+
+        def quantize_y(i):
+            c = slice(i * TOK, (i + 1) * TOK)
+            nc.vector.quantize_mx(out=y_codes[:, c].bitcast(FP8X4), scales=y_planes[:, c], in_=y_mid[:, i * E:(i + 1) * E])
+
+        def permute_scales(w, g):
+            c = slice(g * 512, (g + 1) * 512)
+            nc.vector.tensor_copy(out=w_perm_sc[w][:, c].rearrange("p (t m) -> p t m", t=T), in_=w_raw_sc[w][:, c].rearrange("p (m t) -> p t m", t=T))
+
+        def permute_codes(w, g):
+            c = slice(g * 1024, (g + 1) * 1024)
+            nc.vector.tensor_copy(out=w_perm[w][:, c].rearrange("p (t m b) -> p t m b", t=T, b=2), in_=w_raw[w][:, c].rearrange("p (m t b) -> p t m b", t=T, b=2))
+
+        def turn_first(i):
+            ps = psum.tile([P, 4 * TOK], F32, name="f_ps", tag="f_ps", bufs=1)
+            src = f_rows[i][:].bitcast(F32)
+            for g in range(G):
+                for u in range(2):
+                    k = 2 * g + u
+                    nc.tensor.transpose(ps[:, k * TOK:(k + 1) * TOK], src[:, 256 * g + u:256 * (g + 1):2], ident[:])
+            return ps
+
+        def multiply(i, w, g):
+            ps = psum.tile([P, T * TOK], F32, name="s_ps", tag="s_ps", bufs=3)
+            tok = slice(i * TOK, (i + 1) * TOK)
+            for t in range(T):
+                n = g * T + t
+                nc.tensor.matmul_mx(
+                    out=ps[:, t * TOK:(t + 1) * TOK],
+                    lhsT=w_perm[w][:, n * 256:(n + 1) * 256].bitcast(FP4X4), lhsT_scale=w_perm_sc[w][:, n * P:(n + 1) * P],
+                    rhs=y_codes[:, tok].bitcast(FP8X4), rhs_scale=y_planes[:, tok], start=True, stop=True)
+            return ps
+
+        def relu(w, g, ps):
+            r = work.tile([P, T * TOK], F32, name=f"relu{w}", tag=f"relu{w}", bufs=4)
+            for t in range(T):
+                c = slice(t * TOK, (t + 1) * TOK)
+                nc.scalar.activation(out=r[:, c], in_=ps[:, c], func=RELU, bias=bias[w][:, g * T + t:g * T + t + 1])
+            return r
+
+        def gate(g, s, f_ps):
+            q = work.tile([P, TOK * T], F32, name="q", tag="q", bufs=4)
+            nc.vector.tensor_tensor(
+                out=q[:].rearrange("p (r u e) -> p r u e", u=2, e=2),
+                in0=s[:].rearrange("p (u e r) -> p r u e", u=2, e=2),
+                in1=f_ps[:, g * 2 * TOK:(g + 1) * 2 * TOK].bitcast(BF16).rearrange("p (u r e) -> p r u e", u=2, e=2),
+                op=MULT)
+            return q
+
+        def fuse(engine, i, g, q, inter):
+            engine.tensor_tensor(
+                out=z_mid[i][:, g * 512:(g + 1) * 512].rearrange("p (r t) -> p r t", t=T),
+                in0=q[:].rearrange("p (r t) -> p r t", t=T),
+                in1=inter[:].rearrange("p (t r) -> p r t", t=T),
+                op=ADD)
+
+        def quantize_z(i):
+            nc.vector.quantize_mx(out=z_codes[i][:].bitcast(FP8X4), scales=z_planes[i][:], in_=z_mid[i][:])
+
+        def head(i, j):
+            ps = bank("o_ps", [P, NB], F32)
+            for g in range(G):
+                c = slice(g * TOK, (g + 1) * TOK)
+                n = g * V + j * NB
+                nc.tensor.matmul_mx(
+                    out=ps[:], lhsT=z_codes[i][:, c].bitcast(FP8X4), lhsT_scale=z_planes[i][:, c],
+                    rhs=wo[:, 2 * n:2 * (n + NB)].bitcast(FP4X4), rhs_scale=wo_sc[:, n:n + NB],
+                    start=(g == 0), stop=(g == G - 1))
+            return ps
+
+        def finish(i, j, ps, helped):
+            c = slice(j * NB, (j + 1) * NB)
+            o = o_tiles[i]
+            if helped:
+                nc.scalar.copy(out=o[:, c], in_=ps[:])
+                nc.gpsimd.tensor_tensor(out=o[:, c], in0=o[:, c], in1=b_all[:, c], op=ADD)
+            else:
+                nc.vector.tensor_tensor(out=o[:, c], in0=ps[:], in1=b_all[:, c], op=ADD)
+            width = 1 if i == TILES - 1 and j >= 6 else 2
+            if (j + 1) % width == 0:
+                c = slice((j + 1 - width) * NB, (j + 1) * NB)
+                nc.sync.dma_start(out=out[i * TOK:(i + 1) * TOK, c], in_=o[:, c])
+
+        widen(0)
+        y0 = turn_y(0)
+        permute_codes(0, 0)
+        scale_y(0, y0)
+        permute_scales(0, 0)
+        quantize_y(0)
+        permute_codes(0, 1)
+        permute_scales(0, 1)
+        widen(1)
+        parts = {}
+        parts[0, 0] = relu(0, 0, multiply(0, 0, 0))
+        b0 = spread_bias(0)
+        copy_bias(0, b0)
+        parts[0, 1] = relu(0, 1, multiply(0, 0, 1))
+        f0 = turn_first(0)
+        y1 = turn_y(1)
+        permute_codes(1, 0)
+        permute_scales(1, 0)
+        parts[1, 0] = relu(1, 0, multiply(0, 1, 0))
+        permute_codes(1, 1)
+        permute_scales(1, 1)
+        parts[1, 1] = relu(1, 1, multiply(0, 1, 1))
+        copy_bias(1, spread_bias(1))
+        q0 = gate(0, parts[0, 0], f0)
+        q1 = gate(1, parts[0, 1], f0)
+        scale_y(1, y1)
+        fuse(nc.gpsimd, 0, 0, q0, parts[1, 0])
+        fuse(nc.vector, 0, 1, q1, parts[1, 1])
+        quantize_y(1)
+        quantize_z(0)
+        copy_bias(2, spread_bias(2))
+        copy_bias(3, spread_bias(3))
+        widen(2, 2)
+
+        part = {}
+        for s in range(-1, TILES * BANKS):
+            i, j = divmod(s, BANKS)
+            if s >= 0:
+                finish(i, j, head(i, j), helped=(s < 24 and j in (2, 6)))
+            if s in (1, 3):
+                k = 2 + s // 2
+                scale_y(k, turn_y(k))
+                quantize_y(k)
+            for n in range(1, TILES):
+                e = s - (BANKS * (n - 1) - 1)
+                if e == 0:
+                    part["f"] = turn_first(n)
+                    part[0, 0] = relu(0, 0, multiply(n, 0, 0))
+                if e == 1:
+                    part[0, 1] = relu(0, 1, multiply(n, 0, 1))
+                if e == 2:
+                    part[1, 0] = relu(1, 0, multiply(n, 1, 0))
+                    qa = gate(0, part[0, 0], part["f"])
+                if e == 3:
+                    part[1, 1] = relu(1, 1, multiply(n, 1, 1))
+                    qb = gate(1, part[0, 1], part["f"])
+                    fuse(nc.gpsimd, n, 0, qa, part[1, 0])
+                if e == 5:
+                    fuse(nc.vector, n, 1, qb, part[1, 1])
+                if e == 6:
+                    quantize_z(n)

@@ -24,6 +24,13 @@ G = M // 512
 NB = 512
 BANKS = V // NB
 
+HEAD = "pcode00 widen0 pscale00 widen1 turny0 pscale01 turny1 scaley0 turnf0 spread0 pcode01 scaley1 bcopy0 quanty0 pcode10 a00 pcode11 spread1 pscale10 a10 bcopy1 pscale11 c00 gate10 gate00 quanty1 c10 fuse00 fuse10 quantz0".split()
+LATE = {"spread2": -10, "bcopy2": 3.5, "spread3": -13.4, "bcopy3": -3, "widen2": -3.5, "widen3": -14.1, "turny2": 1.8, "scaley2": 1.8, "quanty2": 2.2, "turny3": 6.2, "scaley3": 6.9, "quanty3": 9.9}
+SLOT = {"turnf": -3.3, "a0": -4.2, "a1": -0.9, "c0": 2.1, "c1": 3, "gate0": -1.4, "gate1": 2.6, "fuse0": 3.5, "fuse1": 3.4, "quantz": 5}
+HELP = ()
+YS = "vsvs"
+GF = ("vv", "vv", "vv", "vv")
+
 FLOPS = 2 * ROWS * E * M * 2 + 2 * ROWS * M * V
 
 
@@ -67,42 +74,40 @@ def tile_smcrossbaby_1_pb_w4_kernel(tc, y2_bytes, y2_scale, first, w_second_word
         nc.vector.memset(b_rows[:], 0.0)
         nc.vector.memset(w_raw_sc[0][:].bitcast(I32), 0)
         nc.vector.memset(w_raw_sc[1][:].bitcast(I32), 0)
+        nc.vector.memset(wo_sc[:].bitcast(I32), 0)
         nc.scalar.activation(out=dummy[:, 1:2], in_=dummy[:, 0:1], func=RELU)
 
-        yb = y2_bytes.rearrange("(i p) k -> p i k", p=P)
-        nc.sync.dma_start(out=y_bytes[:, 0:E], in_=y2_bytes[0:P, :])
-        nc.scalar.dma_start(out=y_scale[:], in_=y2_scale.rearrange("o (p t) -> p (o t)", t=T))
         words = (w_second_words, w_int_words)
         scales = (w_second_scales, w_int_scales)
+        biases = (b_second, b_int)
 
-        def load_w(w):
+        def load_first(i, queue):
+            queue.dma_start(out=f_rows[i][:], in_=first[i * TOK:(i + 1) * TOK, :])
+
+        def load_bias(w):
+            nc.gpsimd.dma_start(out=bias16[w][:].rearrange("p (g t) -> p g t", g=G), in_=biases[w].rearrange("(g p t) -> p g t", p=P, t=T))
+
+        nc.scalar.dma_start(out=y_scale[:], in_=y2_scale.rearrange("o (p t) -> p (o t)", t=T))
+        nc.sync.dma_start(out=y_bytes[:].rearrange("p (i k) -> p i k", k=E), in_=y2_bytes.rearrange("(i p) k -> p i k", p=P))
+        for w in range(2):
             nc.sync.dma_start(out=w_raw[w][:].bitcast(I32), in_=words[w][0].bitcast(I32))
+        for w in range(2):
             for r in range(4):
                 nc.sync.dma_start(out=w_raw_sc[w][r:P:32, :].bitcast(I32), in_=scales[w][0][r:16:4, :].bitcast(I32))
-
-        load_w(0)
-        nc.sync.dma_start(out=y_bytes[:, E:].rearrange("p (i k) -> p i k", k=E), in_=yb[:, 1:, :])
-        load_w(1)
-        nc.gpsimd.dma_start(out=bias16[0][:].rearrange("p (g t) -> p g t", g=G), in_=b_second.rearrange("(g p t) -> p g t", p=P, t=T))
-        make_identity(nc, ident[:])
-        nc.gpsimd.dma_start(out=b_rows[0:BANKS, :], in_=b_out.rearrange("(j n) -> j n", j=BANKS))
-        nc.gpsimd.dma_start(out=bias16[1][:].rearrange("p (g t) -> p g t", g=G), in_=b_int.rearrange("(g p t) -> p g t", p=P, t=T))
-        nc.gpsimd.memset(wo_sc[:].bitcast(I32), 0)
-
-        def load_first(i):
-            nc.sync.dma_start(out=f_rows[i][:], in_=first[i * TOK:(i + 1) * TOK, :])
-
-        load_first(0)
-        load_first(1)
         src_sc = w_out_scales.bitcast(I32).rearrange("g (q r) n -> r q g n", r=4)
         for r in range(4):
             nc.sync.dma_start(out=wo_sc[r:P:32, :].bitcast(I32).rearrange("p (g n) -> p g n", g=G), in_=src_sc[r])
         src_wo = w_out_words.bitcast(I32).rearrange("g p n -> p g n")
         dst_wo = wo[:].bitcast(I32).rearrange("p (g n) -> p g n", g=G)
         for c in range(4):
+            if c > 0:
+                load_first(c, nc.sync)
             nc.sync.dma_start(out=dst_wo[:, :, c * 512:(c + 1) * 512], in_=src_wo[:, :, c * 512:(c + 1) * 512])
-            if c < 2:
-                load_first(2 + c)
+        load_bias(0)
+        make_identity(nc, ident[:])
+        load_first(0, nc.gpsimd)
+        nc.gpsimd.dma_start(out=b_rows[0:BANKS, :], in_=b_out.rearrange("(j n) -> j n", j=BANKS))
+        load_bias(1)
 
         nc.scalar.copy(out=ident16[:], in_=ident[:])
         for w in range(2):
@@ -137,6 +142,14 @@ def tile_smcrossbaby_1_pb_w4_kernel(tc, y2_bytes, y2_scale, first, w_second_word
                 in0=ps[:].bitcast(BF16).rearrange("p (u r e) -> p r u e", u=2, e=2),
                 in1=y_scale[:].rearrange("p (u e) -> p u e", e=2).unsqueeze(1).to_broadcast([P, TOK, 2, 2]),
                 op=MULT)
+
+        def scale_y_s(i, ps):
+            src = ps[:].bitcast(BF16).rearrange("p (u r e) -> p u e r", u=2, e=2)
+            dst = y_mid[:, i * E:(i + 1) * E].rearrange("p (r u e) -> p u e r", u=2, e=2)
+            for u in range(2):
+                for e in range(2):
+                    t = 2 * u + e
+                    nc.scalar.activation(out=dst[:, u, e, :], in_=src[:, u, e, :], func=mybir.ActivationFunctionType.Copy, scale=y_scale[:, t:t + 1])
 
         def quantize_y(i):
             c = slice(i * TOK, (i + 1) * TOK)
@@ -220,64 +233,55 @@ def tile_smcrossbaby_1_pb_w4_kernel(tc, y2_bytes, y2_scale, first, w_second_word
                 c = slice((j + 1 - width) * NB, (j + 1) * NB)
                 nc.sync.dma_start(out=out[i * TOK:(i + 1) * TOK, c], in_=o[:, c])
 
-        widen(0)
-        y0 = turn_y(0)
-        permute_codes(0, 0)
-        scale_y(0, y0)
-        permute_scales(0, 0)
-        quantize_y(0)
-        permute_codes(0, 1)
-        permute_scales(0, 1)
-        widen(1)
-        parts = {}
-        parts[0, 0] = relu(0, 0, multiply(0, 0, 0))
-        b0 = spread_bias(0)
-        copy_bias(0, b0)
-        parts[0, 1] = relu(0, 1, multiply(0, 0, 1))
-        f0 = turn_first(0)
-        y1 = turn_y(1)
-        permute_codes(1, 0)
-        permute_scales(1, 0)
-        parts[1, 0] = relu(1, 0, multiply(0, 1, 0))
-        permute_codes(1, 1)
-        permute_scales(1, 1)
-        parts[1, 1] = relu(1, 1, multiply(0, 1, 1))
-        copy_bias(1, spread_bias(1))
-        q0 = gate(0, parts[0, 0], f0)
-        q1 = gate(1, parts[0, 1], f0)
-        scale_y(1, y1)
-        fuse(nc.gpsimd, 0, 0, q0, parts[1, 0])
-        fuse(nc.vector, 0, 1, q1, parts[1, 1])
-        quantize_y(1)
-        quantize_z(0)
-        copy_bias(2, spread_bias(2))
-        copy_bias(3, spread_bias(3))
-        widen(2, 2)
+        hold = {}
+        plan = []
 
-        part = {}
-        for s in range(-1, TILES * BANKS):
-            i, j = divmod(s, BANKS)
-            if s >= 0:
-                finish(i, j, head(i, j), helped=(s < 24 and j in (2, 6)))
-            if s in (1, 3):
-                k = 2 + s // 2
-                scale_y(k, turn_y(k))
-                quantize_y(k)
-            for n in range(1, TILES):
-                e = s - (BANKS * (n - 1) - 1)
-                if e == 0:
-                    part["f"] = turn_first(n)
-                    part[0, 0] = relu(0, 0, multiply(n, 0, 0))
-                if e == 1:
-                    part[0, 1] = relu(0, 1, multiply(n, 0, 1))
-                if e == 2:
-                    part[1, 0] = relu(1, 0, multiply(n, 1, 0))
-                    qa = gate(0, part[0, 0], part["f"])
-                if e == 3:
-                    part[1, 1] = relu(1, 1, multiply(n, 1, 1))
-                    qb = gate(1, part[0, 1], part["f"])
-                    fuse(nc.gpsimd, n, 0, qa, part[1, 0])
-                if e == 5:
-                    fuse(nc.vector, n, 1, qb, part[1, 1])
-                if e == 6:
-                    quantize_z(n)
+        def ev(name):
+            if name[:5] == "widen":
+                n = int(name[5:])
+                widen(n)
+            elif name[:5] == "turny":
+                hold[name] = turn_y(int(name[5:]))
+            elif name[:6] == "scaley":
+                n = name[6:]
+                (scale_y if YS[int(n)] == "v" else scale_y_s)(int(n), hold["turny" + n])
+            elif name[:6] == "quanty":
+                quantize_y(int(name[6:]))
+            elif name[:5] == "pcode":
+                permute_codes(int(name[5]), int(name[6]))
+            elif name[:6] == "pscale":
+                permute_scales(int(name[6]), int(name[7]))
+            elif name[:6] == "spread":
+                hold[name] = spread_bias(int(name[6:]))
+            elif name[:5] == "bcopy":
+                copy_bias(int(name[5:]), hold["spread" + name[5:]])
+            elif name[:5] == "turnf":
+                hold[name] = turn_first(int(name[5:]))
+            elif name[:4] == "gate":
+                g, n = name[4], name[5]
+                hold["q" + g + n] = gate(int(g), hold["a" + g + n], hold["turnf" + n])
+            elif name[:4] == "fuse":
+                g, n = name[4], name[5]
+                fuse(nc.gpsimd if GF[int(n)][int(g)] == "g" else nc.vector, int(n), int(g), hold["q" + g + n], hold["c" + g + n])
+            elif name[:6] == "quantz":
+                quantize_z(int(name[6:]))
+            elif name[0] in "ac":
+                w = 0 if name[0] == "a" else 1
+                g, n = name[1], name[2]
+                hold[name] = relu(w, int(g), multiply(int(n), w, int(g)))
+
+        for k, name in enumerate(HEAD):
+            plan.append((k - 100.0, name))
+        for name, key in LATE.items():
+            plan.append((key, name))
+        for n in range(1, TILES):
+            for name, key in SLOT.items():
+                plan.append((key + BANKS * (n - 1), name + str(n)))
+        for s in range(TILES * BANKS):
+            plan.append((float(s), s))
+        for key, name in sorted(plan, key=lambda x: x[0]):
+            if isinstance(name, int):
+                i, j = divmod(name, BANKS)
+                finish(i, j, head(i, j), helped=(name in HELP))
+            else:
+                ev(name)

@@ -24,12 +24,12 @@ G = M // 512
 NB = 512
 BANKS = V // NB
 
-HEAD = "pcode00 widen0 pscale00 widen1 turny0 pscale01 turny1 scaley0 turnf0 spread0 pcode01 scaley1 bcopy0 quanty0 pcode10 a00 pcode11 spread1 pscale10 a10 bcopy1 pscale11 c00 gate10 gate00 quanty1 c10 fuse00 fuse10 quantz0".split()
-LATE = {"spread2": -10, "bcopy2": 3.5, "spread3": -13.4, "bcopy3": -3, "widen2": -3.5, "widen3": -14.1, "turny2": 1.8, "scaley2": 1.8, "quanty2": 2.2, "turny3": 6.2, "scaley3": 6.9, "quanty3": 9.9}
-SLOT = {"turnf": -3.3, "a0": -4.2, "a1": -0.9, "c0": 2.1, "c1": 3, "gate0": -1.4, "gate1": 2.6, "fuse0": 3.5, "fuse1": 3.4, "quantz": 5}
-HELP = ()
-YS = "vsvs"
-GF = ("vv", "vv", "vv", "vv")
+HEAD = "pcode00 widen0 turny0 scaley0 pscale01 quanty0 tbias pcode01 turnf0 pcode11 widen1 a10 pscale00 pcode10 pscale10 spread0 pscale11 a00 bcopy0 gate10 gate00 turny1 scaley1 spread1 c00 fuse00 c10 quanty1 bcopy1 fuse10 quantz0".split()
+LATE = {"spread2": -3.7, "bcopy2": 3.7, "spread3": -8, "bcopy3": -4.4, "widen2": -1.7, "widen3": -14.5, "turny2": 1.2, "scaley2": 1.4, "quanty2": 1.6, "turny3": 0.3, "scaley3": 4, "quanty3": 5}
+SLOT = {"turnf": -3, "a0": -1.8, "a1": -0.6, "c0": -0.8, "c1": 1.8, "gate0": -0.1, "gate1": 1.4, "fuse0": 1, "fuse1": 3, "quantz": 5.3}
+HELP = {2, 5, 14}
+YS = "vvvv"
+GF = ("vv", "gv", "gg", "gg")
 
 FLOPS = 2 * ROWS * E * M * 2 + 2 * ROWS * M * V
 
@@ -61,8 +61,8 @@ def tile_smcrossbaby_1_pb_w4_kernel(tc, y2_bytes, y2_scale, first, w_second_word
         w_raw_sc = [sb(f"w_raw_sc{w}", M, U8) for w in range(2)]
         w_perm = [sb(f"w_perm{w}", 2 * M, U8) for w in range(2)]
         w_perm_sc = [sb(f"w_perm_sc{w}", M, U8) for w in range(2)]
-        bias16 = [sb(f"bias16_{w}", G * T, BF16) for w in range(2)]
-        bias = [sb(f"bias_{w}", G * T, F32) for w in range(2)]
+        bias_rows = sb("bias_rows", 512, BF16)
+        bias = sb("bias", T * 2 * G, F32)
         wo = sb("wo", G * 2 * V, U8)
         wo_sc = sb("wo_sc", G * V, U8)
         z_mid = [sb(f"z_mid{i}", G * TOK * T, BF16) for i in range(TILES)]
@@ -70,30 +70,31 @@ def tile_smcrossbaby_1_pb_w4_kernel(tc, y2_bytes, y2_scale, first, w_second_word
         z_planes = [sb(f"z_planes{i}", G * TOK, U8) for i in range(TILES)]
         o_tiles = [sb(f"o{i}", V, F32) for i in range(TILES)]
 
+        nc.vector.memset(w_raw_sc[0][:].bitcast(I32), 0)
         nc.vector.memset(dummy[:], 0.0)
         nc.vector.memset(b_rows[:], 0.0)
-        nc.vector.memset(w_raw_sc[0][:].bitcast(I32), 0)
+        nc.vector.memset(bias_rows[:], 0.0)
         nc.vector.memset(w_raw_sc[1][:].bitcast(I32), 0)
         nc.vector.memset(wo_sc[:].bitcast(I32), 0)
         nc.scalar.activation(out=dummy[:, 1:2], in_=dummy[:, 0:1], func=RELU)
 
         words = (w_second_words, w_int_words)
         scales = (w_second_scales, w_int_scales)
-        biases = (b_second, b_int)
 
         def load_first(i, queue):
             queue.dma_start(out=f_rows[i][:], in_=first[i * TOK:(i + 1) * TOK, :])
 
-        def load_bias(w):
-            nc.gpsimd.dma_start(out=bias16[w][:].rearrange("p (g t) -> p g t", g=G), in_=biases[w].rearrange("(g p t) -> p g t", p=P, t=T))
-
-        nc.scalar.dma_start(out=y_scale[:], in_=y2_scale.rearrange("o (p t) -> p (o t)", t=T))
-        nc.sync.dma_start(out=y_bytes[:].rearrange("p (i k) -> p i k", k=E), in_=y2_bytes.rearrange("(i p) k -> p i k", p=P))
-        for w in range(2):
-            nc.sync.dma_start(out=w_raw[w][:].bitcast(I32), in_=words[w][0].bitcast(I32))
-        for w in range(2):
+        def load_scales(w):
             for r in range(4):
                 nc.sync.dma_start(out=w_raw_sc[w][r:P:32, :].bitcast(I32), in_=scales[w][0][r:16:4, :].bitcast(I32))
+
+        nc.sync.dma_start(out=y_bytes[:, 0:E], in_=y2_bytes[0:P, :])
+        nc.scalar.dma_start(out=y_scale[:], in_=y2_scale.rearrange("o (p t) -> p (o t)", t=T))
+        load_scales(0)
+        for w in range(2):
+            nc.sync.dma_start(out=w_raw[w][:].bitcast(I32), in_=words[w][0].bitcast(I32))
+        load_scales(1)
+        nc.sync.dma_start(out=y_bytes[:, E:].rearrange("p (i k) -> p i k", k=E), in_=y2_bytes.rearrange("(i p) k -> p i k", p=P)[:, 1:, :])
         src_sc = w_out_scales.bitcast(I32).rearrange("g (q r) n -> r q g n", r=4)
         for r in range(4):
             nc.sync.dma_start(out=wo_sc[r:P:32, :].bitcast(I32).rearrange("p (g n) -> p g n", g=G), in_=src_sc[r])
@@ -103,21 +104,25 @@ def tile_smcrossbaby_1_pb_w4_kernel(tc, y2_bytes, y2_scale, first, w_second_word
             if c > 0:
                 load_first(c, nc.sync)
             nc.sync.dma_start(out=dst_wo[:, :, c * 512:(c + 1) * 512], in_=src_wo[:, :, c * 512:(c + 1) * 512])
-        load_bias(0)
         make_identity(nc, ident[:])
+        for w, b in enumerate((b_second, b_int)):
+            nc.gpsimd.dma_start(out=bias_rows[2 * w:2 * w + 2, :], in_=b.rearrange("(g n) -> g n", g=G))
         load_first(0, nc.gpsimd)
         nc.gpsimd.dma_start(out=b_rows[0:BANKS, :], in_=b_out.rearrange("(j n) -> j n", j=BANKS))
-        load_bias(1)
 
         nc.scalar.copy(out=ident16[:], in_=ident[:])
-        for w in range(2):
-            nc.gpsimd.tensor_copy(out=bias[w][:], in_=bias16[w][:])
 
         def widen(i, n=1):
             nc.scalar.copy(out=y_wide[:, i * E:(i + n) * E], in_=y_bytes[:, i * E:(i + n) * E].bitcast(FP8))
 
         def bank(name, shape, dtype):
             return psum.tile(shape, dtype, name=name, tag="wide", bufs=4)
+
+        def turn_bias():
+            ps = bank("bias_ps", [P, T * P], BF16)
+            for t in range(T):
+                nc.tensor.transpose(ps[:, t * P:(t + 1) * P], bias_rows[:, t:512:T], ident16[:])
+            nc.scalar.copy(out=bias[:].rearrange("p (t x) -> p t x", t=T), in_=ps[:].rearrange("p (t x) -> p t x", t=T)[:, :, 0:2 * G])
 
         def spread_bias(h):
             ps = bank("b_ps", [P, 2 * NB], BF16)
@@ -187,23 +192,23 @@ def tile_smcrossbaby_1_pb_w4_kernel(tc, y2_bytes, y2_scale, first, w_second_word
             r = work.tile([P, T * TOK], F32, name=f"relu{w}", tag=f"relu{w}", bufs=4)
             for t in range(T):
                 c = slice(t * TOK, (t + 1) * TOK)
-                nc.scalar.activation(out=r[:, c], in_=ps[:, c], func=RELU, bias=bias[w][:, g * T + t:g * T + t + 1])
+                nc.scalar.activation(out=r[:, c], in_=ps[:, c], func=RELU, bias=bias[:, (t * 2 + w) * G + g:(t * 2 + w) * G + g + 1])
             return r
 
         def gate(g, s, f_ps):
             q = work.tile([P, TOK * T], F32, name="q", tag="q", bufs=4)
             nc.vector.tensor_tensor(
-                out=q[:].rearrange("p (r u e) -> p r u e", u=2, e=2),
-                in0=s[:].rearrange("p (u e r) -> p r u e", u=2, e=2),
-                in1=f_ps[:, g * 2 * TOK:(g + 1) * 2 * TOK].bitcast(BF16).rearrange("p (u r e) -> p r u e", u=2, e=2),
+                out=q[:].rearrange("p (u e r) -> p u e r", u=2, e=2),
+                in0=s[:].rearrange("p (u e r) -> p u e r", u=2, e=2),
+                in1=f_ps[:, g * 2 * TOK:(g + 1) * 2 * TOK].bitcast(BF16).rearrange("p (u r e) -> p u e r", u=2, e=2),
                 op=MULT)
             return q
 
         def fuse(engine, i, g, q, inter):
             engine.tensor_tensor(
-                out=z_mid[i][:, g * 512:(g + 1) * 512].rearrange("p (r t) -> p r t", t=T),
-                in0=q[:].rearrange("p (r t) -> p r t", t=T),
-                in1=inter[:].rearrange("p (t r) -> p r t", t=T),
+                out=z_mid[i][:, g * 512:(g + 1) * 512].rearrange("p (c i t) -> p c t i", i=4, t=T),
+                in0=q[:].rearrange("p (t c i) -> p c t i", t=T, i=4),
+                in1=inter[:].rearrange("p (t c i) -> p c t i", t=T, i=4),
                 op=ADD)
 
         def quantize_z(i):
@@ -251,6 +256,8 @@ def tile_smcrossbaby_1_pb_w4_kernel(tc, y2_bytes, y2_scale, first, w_second_word
                 permute_codes(int(name[5]), int(name[6]))
             elif name[:6] == "pscale":
                 permute_scales(int(name[6]), int(name[7]))
+            elif name == "tbias":
+                turn_bias()
             elif name[:6] == "spread":
                 hold[name] = spread_bias(int(name[6:]))
             elif name[:5] == "bcopy":

@@ -24,12 +24,12 @@ G = M // 512
 NB = 512
 BANKS = V // NB
 
-HEAD = "pcode00 widen0 turny0 scaley0 pscale01 quanty0 tbias pcode01 turnf0 pcode11 widen1 a10 pscale00 pcode10 pscale10 spread0 pscale11 a00 bcopy0 gate10 gate00 turny1 scaley1 spread1 c00 fuse00 c10 quanty1 bcopy1 fuse10 quantz0".split()
-LATE = {"spread2": -3.7, "bcopy2": 3.7, "spread3": -8, "bcopy3": -4.4, "widen2": -1.7, "widen3": -14.5, "turny2": 1.2, "scaley2": 1.4, "quanty2": 1.6, "turny3": 0.3, "scaley3": 4, "quanty3": 5}
-SLOT = {"turnf": -3, "a0": -1.8, "a1": -0.6, "c0": -0.8, "c1": 1.8, "gate0": -0.1, "gate1": 1.4, "fuse0": 1, "fuse1": 3, "quantz": 5.3}
+HEAD = "pcode00 widen0 pcode01 pscale00 turny0 scaley0 tbias pscale01 quanty0 pcode10 a00 pcode11 a10 pscale10 widen1 turnf0 pscale11 gate00 spread0 gate10 c00 fuse00 bcopy0 spread1 c10 bcopy1 turny1 scaley1 quanty1 fuse10 quantz0".split()
+LATE = {"spread2": -17, "bcopy2": 1.5, "spread3": -15.3, "bcopy3": -9.6, "widen2": -1.6, "widen3": -8.5, "turny2": 0.8, "scaley2": 0.8, "quanty2": 2, "turny3": 0.5, "scaley3": 4, "quanty3": 5.7}
+SLOT = {"turnf": -4.2, "a0": -3.7, "a1": -0.4, "c0": -1.6, "c1": 0.3, "gate0": -1.8, "gate1": 0.9, "fuse0": -0.3, "fuse1": 2, "quantz": 6}
 HELP = {2, 5, 14}
 YS = "vvvv"
-GF = ("vv", "gv", "gg", "gg")
+GF = ("gv", "gv", "gg", "gg")
 
 FLOPS = 2 * ROWS * E * M * 2 + 2 * ROWS * M * V
 
@@ -81,19 +81,26 @@ def tile_smcrossbaby_1_pb_w4_kernel(tc, y2_bytes, y2_scale, first, w_second_word
         words = (w_second_words, w_int_words)
         scales = (w_second_scales, w_int_scales)
 
-        def load_first(i, queue):
-            queue.dma_start(out=f_rows[i][:], in_=first[i * TOK:(i + 1) * TOK, :])
+        def load_first(i):
+            nc.sync.dma_start(out=f_rows[i][:], in_=first[i * TOK:(i + 1) * TOK, :])
 
         def load_scales(w):
             for r in range(4):
                 nc.sync.dma_start(out=w_raw_sc[w][r:P:32, :].bitcast(I32), in_=scales[w][0][r:16:4, :].bitcast(I32))
 
+        def load_words(w):
+            nc.sync.dma_start(out=w_raw[w][:].bitcast(I32), in_=words[w][0].bitcast(I32))
+
+        load_words(0)
         nc.sync.dma_start(out=y_bytes[:, 0:E], in_=y2_bytes[0:P, :])
         nc.scalar.dma_start(out=y_scale[:], in_=y2_scale.rearrange("o (p t) -> p (o t)", t=T))
         load_scales(0)
-        for w in range(2):
-            nc.sync.dma_start(out=w_raw[w][:].bitcast(I32), in_=words[w][0].bitcast(I32))
+        load_words(1)
+        for w, b in enumerate((b_second, b_int)):
+            nc.sync.dma_start(out=bias_rows[2 * w:2 * w + 2, :], in_=b.rearrange("(g n) -> g n", g=G))
         load_scales(1)
+        load_first(0)
+        nc.sync.dma_start(out=b_rows[0:BANKS, :], in_=b_out.rearrange("(j n) -> j n", j=BANKS))
         nc.sync.dma_start(out=y_bytes[:, E:].rearrange("p (i k) -> p i k", k=E), in_=y2_bytes.rearrange("(i p) k -> p i k", p=P)[:, 1:, :])
         src_sc = w_out_scales.bitcast(I32).rearrange("g (q r) n -> r q g n", r=4)
         for r in range(4):
@@ -102,13 +109,9 @@ def tile_smcrossbaby_1_pb_w4_kernel(tc, y2_bytes, y2_scale, first, w_second_word
         dst_wo = wo[:].bitcast(I32).rearrange("p (g n) -> p g n", g=G)
         for c in range(4):
             if c > 0:
-                load_first(c, nc.sync)
+                load_first(c)
             nc.sync.dma_start(out=dst_wo[:, :, c * 512:(c + 1) * 512], in_=src_wo[:, :, c * 512:(c + 1) * 512])
         make_identity(nc, ident[:])
-        for w, b in enumerate((b_second, b_int)):
-            nc.gpsimd.dma_start(out=bias_rows[2 * w:2 * w + 2, :], in_=b.rearrange("(g n) -> g n", g=G))
-        load_first(0, nc.gpsimd)
-        nc.gpsimd.dma_start(out=b_rows[0:BANKS, :], in_=b_out.rearrange("(j n) -> j n", j=BANKS))
 
         nc.scalar.copy(out=ident16[:], in_=ident[:])
 

@@ -15,283 +15,348 @@ ADD = mybir.AluOpType.add
 MULT = mybir.AluOpType.mult
 RELU = mybir.ActivationFunctionType.Relu
 
+TOKENS, FEATURES, CHANNELS, OUTPUTS = 512, 512, 1024, 4096
+
 P = 128
-ROWS, E, M, V = 512, 512, 1024, 4096
-T = 4
-TOK = 128
-TILES = ROWS // TOK
-G = M // 512
-NB = 512
-BANKS = V // NB
+PACK = 4
+K_PASS = P * PACK
+PASSES = CHANNELS // K_PASS
+TILE = 128
+TILES = TOKENS // TILE
+BANK = 512
+BLOCKS = OUTPUTS // BANK
+CODE = 2
+SCALE_ROWS = 4
+SECOND, INTER = 0, 1
 
-HEAD = "pcode00 widen0 pcode01 pscale00 turny0 scaley0 tbias pscale01 quanty0 pcode10 a00 pcode11 a10 pscale10 widen1 turnf0 pscale11 gate00 spread0 gate10 c00 fuse00 bcopy0 spread1 c10 bcopy1 turny1 scaley1 quanty1 fuse10 quantz0".split()
-LATE = {"spread2": -17, "bcopy2": 1.5, "spread3": -15.3, "bcopy3": -9.6, "widen2": -1.6, "widen3": -8.5, "turny2": 0.8, "scaley2": 0.8, "quanty2": 2, "turny3": 0.5, "scaley3": 4, "quanty3": 5.7}
-SLOT = {"turnf": -4.2, "a0": -3.7, "a1": -0.4, "c0": -1.6, "c1": 0.3, "gate0": -1.8, "gate1": 0.9, "fuse0": -0.3, "fuse1": 2, "quantz": 6}
-HELP = {2, 5, 14}
-YS = "vvvv"
-GF = ("gv", "gv", "gg", "gg")
+SHARED_BLOCKS = (6, 14)
+WARM_UP_MATMULS = 5
 
-FLOPS = 2 * ROWS * E * M * 2 + 2 * ROWS * M * V
+FLOPS = 2 * TOKENS * FEATURES * CHANNELS * 2 + 2 * TOKENS * CHANNELS * OUTPUTS
 
 
-def tile_smcrossbaby_1_pb_w4_kernel(tc, y2_bytes, y2_scale, first, w_second_words, w_second_scales, b_second, w_int_words, w_int_scales, b_int, w_out_words, w_out_scales, b_out, out):
+def tile_smcrossbaby_1_pb_w4_kernel(
+    tc, y2_bytes, y2_scale, first, w_second_words, w_second_scales, b_second, w_int_words, w_int_scales, b_int,
+    w_out_words, w_out_scales, b_out, out,
+):
     nc = tc.nc
+
     with ExitStack() as ctx:
         keep = ctx.enter_context(tc.tile_pool(name="keep", bufs=1))
         work = ctx.enter_context(tc.tile_pool(name="work", bufs=4))
         psum = ctx.enter_context(tc.psum_pool(name="psum", bufs=1))
         ctx.enter_context(tc.manual_schedule())
 
-        def sb(name, width, dtype):
+        def kept(name, width, dtype):
             return keep.tile([P, width], dtype, name=name, align_bytes=64)
 
-        ident = sb("ident", P, F32)
-        ident16 = sb("ident16", P, BF16)
-        dummy = sb("dummy", 2, F32)
-        b_rows = sb("b_rows", NB, BF16)
-        b_all = sb("b_all", V, BF16)
-        y_bytes = sb("y_bytes", TILES * E, U8)
-        y_wide = sb("y_wide", TILES * E, BF16)
-        y_scale = sb("y_scale", T, F32)
-        y_mid = sb("y_mid", TILES * E, BF16)
-        y_codes = sb("y_codes", ROWS, U32)
-        y_planes = sb("y_planes", ROWS, U8)
-        f_rows = [sb(f"f_rows{i}", M, BF16) for i in range(TILES)]
-        w_raw = [sb(f"w_raw{w}", 2 * M, U8) for w in range(2)]
-        w_raw_sc = [sb(f"w_raw_sc{w}", M, U8) for w in range(2)]
-        w_perm = [sb(f"w_perm{w}", 2 * M, U8) for w in range(2)]
-        w_perm_sc = [sb(f"w_perm_sc{w}", M, U8) for w in range(2)]
-        bias_rows = sb("bias_rows", 512, BF16)
-        bias = sb("bias", T * 2 * G, F32)
-        wo = sb("wo", G * 2 * V, U8)
-        wo_sc = sb("wo_sc", G * V, U8)
-        z_mid = [sb(f"z_mid{i}", G * TOK * T, BF16) for i in range(TILES)]
-        z_codes = [sb(f"z_codes{i}", G * TOK, U32) for i in range(TILES)]
-        z_planes = [sb(f"z_planes{i}", G * TOK, U8) for i in range(TILES)]
-        o_tiles = [sb(f"o{i}", V, F32) for i in range(TILES)]
+        def bank(name, width, dtype):
+            return psum.tile([P, width], dtype, name=name, tag="bank", bufs=4)
 
-        nc.vector.memset(w_raw_sc[0][:].bitcast(I32), 0)
-        nc.vector.memset(dummy[:], 0.0)
-        nc.vector.memset(b_rows[:], 0.0)
+        identity = kept("identity", P, F32)
+        identity_bf16 = kept("identity_bf16", P, BF16)
+        zeros = kept("zeros", BANK, BF16)
+        table_probe = kept("table_probe", 2, F32)
+        y_bytes = kept("y_bytes", TILES * FEATURES, U8)
+        y_values = kept("y_values", TILES * FEATURES, BF16)
+        y_scale = kept("y_scale", PACK, F32)
+        y_packed = kept("y_packed", TOKENS * PACK, BF16)
+        y_codes = kept("y_codes", TOKENS, U32)
+        y_scale_bytes = kept("y_scale_bytes", TOKENS, U8)
+        w_codes = [kept(f"w_codes{w}", CHANNELS * CODE, U8) for w in (SECOND, INTER)]
+        w_scale_bytes = [kept(f"w_scale_bytes{w}", CHANNELS, U8) for w in (SECOND, INTER)]
+        w_codes_by_t = [kept(f"w_codes_by_t{w}", CHANNELS * CODE, U8) for w in (SECOND, INTER)]
+        w_scale_bytes_by_t = [kept(f"w_scale_bytes_by_t{w}", CHANNELS, U8) for w in (SECOND, INTER)]
+        bias_rows = kept("bias_rows", K_PASS, BF16)
+        bias = kept("bias", PACK * 2 * PASSES, F32)
+        first_rows = [kept(f"first_rows{i}", CHANNELS, BF16) for i in range(TILES)]
+        z_packed = [kept(f"z_packed{i}", PASSES * TILE * PACK, BF16) for i in range(TILES)]
+        z_codes = [kept(f"z_codes{i}", PASSES * TILE, U32) for i in range(TILES)]
+        z_scale_bytes = [kept(f"z_scale_bytes{i}", PASSES * TILE, U8) for i in range(TILES)]
+        w_out_codes = kept("w_out_codes", PASSES * OUTPUTS * CODE, U8)
+        w_out_scale_bytes = kept("w_out_scale_bytes", PASSES * OUTPUTS, U8)
+        b_out_rows = kept("b_out_rows", BANK, BF16)
+        b_out_all = kept("b_out_all", OUTPUTS, BF16)
+        out_rows = [kept(f"out_rows{i}", OUTPUTS, F32) for i in range(TILES)]
+
+        nc.vector.memset(b_out_rows[:], 0.0)
+        nc.vector.memset(zeros[:], 0.0)
+        nc.vector.memset(w_scale_bytes[SECOND][:].bitcast(I32), 0)
+        nc.vector.memset(table_probe[:], 0.0)
         nc.vector.memset(bias_rows[:], 0.0)
-        nc.vector.memset(w_raw_sc[1][:].bitcast(I32), 0)
-        nc.vector.memset(wo_sc[:].bitcast(I32), 0)
-        nc.scalar.activation(out=dummy[:, 1:2], in_=dummy[:, 0:1], func=RELU)
+        nc.vector.memset(w_scale_bytes[INTER][:].bitcast(I32), 0)
+        nc.vector.memset(w_out_scale_bytes[:].bitcast(I32), 0)
+        nc.scalar.dma_start(out=b_out_rows[0:BLOCKS, :], in_=b_out.rearrange("(j n) -> j n", j=BLOCKS))
+        nc.scalar.activation(out=table_probe[:, 1:2], in_=table_probe[:, 0:1], func=RELU)
 
         words = (w_second_words, w_int_words)
         scales = (w_second_scales, w_int_scales)
 
-        def load_first(i):
-            nc.sync.dma_start(out=f_rows[i][:], in_=first[i * TOK:(i + 1) * TOK, :])
+        def load_words(w):
+            nc.sync.dma_start(out=w_codes[w][:].bitcast(I32), in_=words[w][0].bitcast(I32))
 
         def load_scales(w):
-            for r in range(4):
-                nc.sync.dma_start(out=w_raw_sc[w][r:P:32, :].bitcast(I32), in_=scales[w][0][r:16:4, :].bitcast(I32))
+            for r in range(SCALE_ROWS):
+                nc.sync.dma_start(
+                    out=w_scale_bytes[w][r:P:32, :].bitcast(I32), in_=scales[w][0][r:16:SCALE_ROWS, :].bitcast(I32)
+                )
 
-        def load_words(w):
-            nc.sync.dma_start(out=w_raw[w][:].bitcast(I32), in_=words[w][0].bitcast(I32))
+        def load_first(i):
+            nc.sync.dma_start(out=first_rows[i][:], in_=first[i * TILE:(i + 1) * TILE, :])
 
-        load_words(0)
-        nc.sync.dma_start(out=y_bytes[:, 0:E], in_=y2_bytes[0:P, :])
-        nc.scalar.dma_start(out=y_scale[:], in_=y2_scale.rearrange("o (p t) -> p (o t)", t=T))
-        load_scales(0)
-        load_words(1)
+        nc.gpsimd.dma_start(out=y_scale[:], in_=y2_scale.rearrange("o (p t) -> p (o t)", t=PACK))
+        make_identity(nc, identity[:])
+        load_words(SECOND)
+        nc.sync.dma_start(out=y_bytes[:, 0:FEATURES], in_=y2_bytes[0:P, :])
+        load_scales(SECOND)
         for w, b in enumerate((b_second, b_int)):
-            nc.sync.dma_start(out=bias_rows[2 * w:2 * w + 2, :], in_=b.rearrange("(g n) -> g n", g=G))
-        load_scales(1)
+            nc.sync.dma_start(
+                out=bias_rows[PASSES * w:PASSES * (w + 1), :], in_=b.rearrange("(g n) -> g n", g=PASSES)
+            )
+        load_words(INTER)
+        nc.sync.dma_start(
+            out=y_bytes[:, FEATURES:].rearrange("p (i k) -> p i k", k=FEATURES),
+            in_=y2_bytes.rearrange("(i p) k -> p i k", p=P)[:, 1:, :],
+        )
+        load_scales(INTER)
         load_first(0)
-        nc.sync.dma_start(out=b_rows[0:BANKS, :], in_=b_out.rearrange("(j n) -> j n", j=BANKS))
-        nc.sync.dma_start(out=y_bytes[:, E:].rearrange("p (i k) -> p i k", k=E), in_=y2_bytes.rearrange("(i p) k -> p i k", p=P)[:, 1:, :])
-        src_sc = w_out_scales.bitcast(I32).rearrange("g (q r) n -> r q g n", r=4)
-        for r in range(4):
-            nc.sync.dma_start(out=wo_sc[r:P:32, :].bitcast(I32).rearrange("p (g n) -> p g n", g=G), in_=src_sc[r])
-        src_wo = w_out_words.bitcast(I32).rearrange("g p n -> p g n")
-        dst_wo = wo[:].bitcast(I32).rearrange("p (g n) -> p g n", g=G)
+        load_first(1)
+        w_out_scale_rows = w_out_scales.bitcast(I32).rearrange("g (q r) n -> r q g n", r=SCALE_ROWS)
+        for r in range(SCALE_ROWS):
+            nc.sync.dma_start(
+                out=w_out_scale_bytes[r:P:32, :].bitcast(I32).rearrange("p (g n) -> p g n", g=PASSES),
+                in_=w_out_scale_rows[r],
+            )
+        w_out_source = w_out_words.bitcast(I32).rearrange("g p n -> p g n")
+        w_out_target = w_out_codes[:].bitcast(I32).rearrange("p (g n) -> p g n", g=PASSES)
+        quarter = OUTPUTS * CODE // 4 // 4
         for c in range(4):
-            if c > 0:
+            if c >= 2:
                 load_first(c)
-            nc.sync.dma_start(out=dst_wo[:, :, c * 512:(c + 1) * 512], in_=src_wo[:, :, c * 512:(c + 1) * 512])
-        make_identity(nc, ident[:])
+            columns = slice(c * quarter, (c + 1) * quarter)
+            nc.sync.dma_start(out=w_out_target[:, :, columns], in_=w_out_source[:, :, columns])
 
-        nc.scalar.copy(out=ident16[:], in_=ident[:])
+        nc.scalar.copy(out=identity_bf16[:], in_=identity[:])
 
-        def widen(i, n=1):
-            nc.scalar.copy(out=y_wide[:, i * E:(i + n) * E], in_=y_bytes[:, i * E:(i + n) * E].bitcast(FP8))
+        def turn_biases():
+            turned = bank("biases_turned", PACK * P, BF16)
+            for t in range(PACK):
+                nc.tensor.transpose(turned[:, t * P:(t + 1) * P], bias_rows[:, t:K_PASS:PACK], identity_bf16[:])
+            nc.scalar.copy(
+                out=bias[:].rearrange("p (t x) -> p t x", t=PACK),
+                in_=turned[:].rearrange("p (t x) -> p t x", t=PACK)[:, :, 0:2 * PASSES],
+            )
 
-        def bank(name, shape, dtype):
-            return psum.tile(shape, dtype, name=name, tag="wide", bufs=4)
-
-        def turn_bias():
-            ps = bank("bias_ps", [P, T * P], BF16)
-            for t in range(T):
-                nc.tensor.transpose(ps[:, t * P:(t + 1) * P], bias_rows[:, t:512:T], ident16[:])
-            nc.scalar.copy(out=bias[:].rearrange("p (t x) -> p t x", t=T), in_=ps[:].rearrange("p (t x) -> p t x", t=T)[:, :, 0:2 * G])
-
-        def spread_bias(h):
-            ps = bank("b_ps", [P, 2 * NB], BF16)
+        def spread_b_out(c):
+            spread = bank("b_out_spread", 2 * BANK, BF16)
             for e in range(2):
-                j = 2 * h + e
-                nc.tensor.matmul(ps[:, e * NB:(e + 1) * NB], lhsT=ident16[:, j:j + 1].to_broadcast([P, P]), rhs=b_rows[:], start=True, stop=True)
-            return ps
+                j = 2 * c + e
+                nc.tensor.matmul(
+                    spread[:, e * BANK:(e + 1) * BANK],
+                    lhsT=identity_bf16[:, j:j + 1].to_broadcast([P, P]),
+                    rhs=b_out_rows[:],
+                    start=True,
+                    stop=True,
+                )
+            return spread
 
-        def copy_bias(h, ps):
-            nc.scalar.copy(out=b_all[:, h * 2 * NB:(h + 1) * 2 * NB], in_=ps[:])
+        def copy_b_out(c, spread):
+            nc.scalar.copy(out=b_out_all[:, c * 2 * BANK:(c + 1) * 2 * BANK], in_=spread[:])
 
-        def turn_y(i):
-            ps = bank("y_ps", [P, 2 * TOK], F32)
-            src = y_wide[:, i * E:(i + 1) * E].bitcast(F32)
-            for u in range(2):
-                nc.tensor.transpose(ps[:, u * TOK:(u + 1) * TOK], src[:, u:2 * P:2], ident[:])
-            return ps
+        def warm_up():
+            sums = psum.tile([P, BANK], F32, name="branch_sums", tag="branch_sums", bufs=3)
+            for k in range(WARM_UP_MATMULS):
+                nc.tensor.matmul(sums[:], lhsT=zeros[:, 0:P], rhs=zeros[:], start=True, stop=True)
 
-        def scale_y(i, ps):
+        def widen_y(i, n):
+            columns = slice(i * FEATURES, (i + n) * FEATURES)
+            nc.scalar.copy(out=y_values[:, columns], in_=y_bytes[:, columns].bitcast(FP8))
+
+        def turn_y(i, n):
+            turned = bank("y_turned", 2 * n * TILE, F32)
+            for k in range(n):
+                pairs = y_values[:, (i + k) * FEATURES:(i + k + 1) * FEATURES].bitcast(F32)
+                for u in range(2):
+                    c = (u * n + k) * TILE
+                    nc.tensor.transpose(turned[:, c:c + TILE], pairs[:, u:2 * P:2], identity[:])
+            return turned
+
+        def scale_y(i, n, turned):
             nc.vector.tensor_tensor(
-                out=y_mid[:, i * E:(i + 1) * E].rearrange("p (r u e) -> p r u e", u=2, e=2),
-                in0=ps[:].bitcast(BF16).rearrange("p (u r e) -> p r u e", u=2, e=2),
-                in1=y_scale[:].rearrange("p (u e) -> p u e", e=2).unsqueeze(1).to_broadcast([P, TOK, 2, 2]),
-                op=MULT)
+                out=y_packed[:, i * TILE * PACK:(i + n) * TILE * PACK].rearrange("p (r u e) -> p r u e", u=2, e=2),
+                in0=turned[:].bitcast(BF16).rearrange("p (u r e) -> p r u e", u=2, e=2),
+                in1=y_scale[:].rearrange("p (u e) -> p u e", e=2).unsqueeze(1).to_broadcast([P, n * TILE, 2, 2]),
+                op=MULT,
+            )
 
-        def scale_y_s(i, ps):
-            src = ps[:].bitcast(BF16).rearrange("p (u r e) -> p u e r", u=2, e=2)
-            dst = y_mid[:, i * E:(i + 1) * E].rearrange("p (r u e) -> p u e r", u=2, e=2)
-            for u in range(2):
-                for e in range(2):
-                    t = 2 * u + e
-                    nc.scalar.activation(out=dst[:, u, e, :], in_=src[:, u, e, :], func=mybir.ActivationFunctionType.Copy, scale=y_scale[:, t:t + 1])
-
-        def quantize_y(i):
-            c = slice(i * TOK, (i + 1) * TOK)
-            nc.vector.quantize_mx(out=y_codes[:, c].bitcast(FP8X4), scales=y_planes[:, c], in_=y_mid[:, i * E:(i + 1) * E])
-
-        def permute_scales(w, g):
-            c = slice(g * 512, (g + 1) * 512)
-            nc.vector.tensor_copy(out=w_perm_sc[w][:, c].rearrange("p (t m) -> p t m", t=T), in_=w_raw_sc[w][:, c].rearrange("p (m t) -> p t m", t=T))
+        def quantize_y(i, n):
+            tokens = slice(i * TILE, (i + n) * TILE)
+            nc.vector.quantize_mx(
+                out=y_codes[:, tokens].bitcast(FP8X4),
+                scales=y_scale_bytes[:, tokens],
+                in_=y_packed[:, i * TILE * PACK:(i + n) * TILE * PACK],
+            )
 
         def permute_codes(w, g):
-            c = slice(g * 1024, (g + 1) * 1024)
-            nc.vector.tensor_copy(out=w_perm[w][:, c].rearrange("p (t m b) -> p t m b", t=T, b=2), in_=w_raw[w][:, c].rearrange("p (m t b) -> p t m b", t=T, b=2))
+            columns = slice(g * K_PASS * CODE, (g + 1) * K_PASS * CODE)
+            nc.vector.tensor_copy(
+                out=w_codes_by_t[w][:, columns].rearrange("p (t m b) -> p t m b", t=PACK, b=CODE),
+                in_=w_codes[w][:, columns].rearrange("p (m t b) -> p t m b", t=PACK, b=CODE),
+            )
+
+        def permute_scales(w, g):
+            columns = slice(g * K_PASS, (g + 1) * K_PASS)
+            nc.vector.tensor_copy(
+                out=w_scale_bytes_by_t[w][:, columns].rearrange("p (t m) -> p t m", t=PACK),
+                in_=w_scale_bytes[w][:, columns].rearrange("p (m t) -> p t m", t=PACK),
+            )
+
+        def branch(i, w, g):
+            sums = psum.tile([P, PACK * TILE], F32, name="branch_sums", tag="branch_sums", bufs=3)
+            tokens = slice(i * TILE, (i + 1) * TILE)
+            for t in range(PACK):
+                n = g * PACK + t
+                nc.tensor.matmul_mx(
+                    out=sums[:, t * TILE:(t + 1) * TILE],
+                    lhsT=w_codes_by_t[w][:, n * P * CODE:(n + 1) * P * CODE].bitcast(FP4X4),
+                    lhsT_scale=w_scale_bytes_by_t[w][:, n * P:(n + 1) * P],
+                    rhs=y_codes[:, tokens].bitcast(FP8X4),
+                    rhs_scale=y_scale_bytes[:, tokens],
+                    start=True,
+                    stop=True,
+                )
+            result = work.tile([P, PACK * TILE], F32, name=f"branch{w}", tag=f"branch{w}", bufs=4)
+            for t in range(PACK):
+                columns = slice(t * TILE, (t + 1) * TILE)
+                b = (t * 2 + w) * PASSES + g
+                nc.scalar.activation(out=result[:, columns], in_=sums[:, columns], func=RELU, bias=bias[:, b:b + 1])
+            return result
 
         def turn_first(i):
-            ps = psum.tile([P, 4 * TOK], F32, name="f_ps", tag="f_ps", bufs=1)
-            src = f_rows[i][:].bitcast(F32)
-            for g in range(G):
+            turned = psum.tile([P, BANK], F32, name="first_turned", tag="first_turned", bufs=1)
+            pairs = first_rows[i][:].bitcast(F32)
+            for g in range(PASSES):
                 for u in range(2):
-                    k = 2 * g + u
-                    nc.tensor.transpose(ps[:, k * TOK:(k + 1) * TOK], src[:, 256 * g + u:256 * (g + 1):2], ident[:])
-            return ps
+                    c = (2 * g + u) * TILE
+                    nc.tensor.transpose(
+                        turned[:, c:c + TILE], pairs[:, 2 * P * g + u:2 * P * (g + 1):2], identity[:]
+                    )
+            return turned
 
-        def multiply(i, w, g):
-            ps = psum.tile([P, T * TOK], F32, name="s_ps", tag="s_ps", bufs=3)
-            tok = slice(i * TOK, (i + 1) * TOK)
-            for t in range(T):
-                n = g * T + t
-                nc.tensor.matmul_mx(
-                    out=ps[:, t * TOK:(t + 1) * TOK],
-                    lhsT=w_perm[w][:, n * 256:(n + 1) * 256].bitcast(FP4X4), lhsT_scale=w_perm_sc[w][:, n * P:(n + 1) * P],
-                    rhs=y_codes[:, tok].bitcast(FP8X4), rhs_scale=y_planes[:, tok], start=True, stop=True)
-            return ps
-
-        def relu(w, g, ps):
-            r = work.tile([P, T * TOK], F32, name=f"relu{w}", tag=f"relu{w}", bufs=4)
-            for t in range(T):
-                c = slice(t * TOK, (t + 1) * TOK)
-                nc.scalar.activation(out=r[:, c], in_=ps[:, c], func=RELU, bias=bias[:, (t * 2 + w) * G + g:(t * 2 + w) * G + g + 1])
-            return r
-
-        def gate(g, s, f_ps):
-            q = work.tile([P, TOK * T], F32, name="q", tag="q", bufs=4)
+        def gate(g, second, first_turned):
+            product = work.tile([P, PACK * TILE], F32, name="product", tag="product", bufs=4)
+            pairs = first_turned[:, g * 2 * TILE:(g + 1) * 2 * TILE].bitcast(BF16)
             nc.vector.tensor_tensor(
-                out=q[:].rearrange("p (u e r) -> p u e r", u=2, e=2),
-                in0=s[:].rearrange("p (u e r) -> p u e r", u=2, e=2),
-                in1=f_ps[:, g * 2 * TOK:(g + 1) * 2 * TOK].bitcast(BF16).rearrange("p (u r e) -> p u e r", u=2, e=2),
-                op=MULT)
-            return q
+                out=product[:].rearrange("p (u e r) -> p u e r", u=2, e=2),
+                in0=second[:].rearrange("p (u e r) -> p u e r", u=2, e=2),
+                in1=pairs.rearrange("p (u r e) -> p u e r", u=2, e=2),
+                op=MULT,
+            )
+            return product
 
-        def fuse(engine, i, g, q, inter):
+        def fuse(engine, i, g, product, inter):
             engine.tensor_tensor(
-                out=z_mid[i][:, g * 512:(g + 1) * 512].rearrange("p (c i t) -> p c t i", i=4, t=T),
-                in0=q[:].rearrange("p (t c i) -> p c t i", t=T, i=4),
-                in1=inter[:].rearrange("p (t c i) -> p c t i", t=T, i=4),
-                op=ADD)
+                out=z_packed[i][:, g * TILE * PACK:(g + 1) * TILE * PACK].rearrange(
+                    "p (c r t) -> p c t r", r=4, t=PACK
+                ),
+                in0=product[:].rearrange("p (t c r) -> p c t r", t=PACK, r=4),
+                in1=inter[:].rearrange("p (t c r) -> p c t r", t=PACK, r=4),
+                op=ADD,
+            )
 
         def quantize_z(i):
-            nc.vector.quantize_mx(out=z_codes[i][:].bitcast(FP8X4), scales=z_planes[i][:], in_=z_mid[i][:])
+            nc.vector.quantize_mx(
+                out=z_codes[i][:].bitcast(FP8X4), scales=z_scale_bytes[i][:], in_=z_packed[i][:]
+            )
 
-        def head(i, j):
-            ps = bank("o_ps", [P, NB], F32)
-            for g in range(G):
-                c = slice(g * TOK, (g + 1) * TOK)
-                n = g * V + j * NB
+        def output_block(s):
+            i, j = divmod(s, BLOCKS)
+            sums = bank("out_sums", BANK, F32)
+            for g in range(PASSES):
+                tokens = slice(g * TILE, (g + 1) * TILE)
+                n = g * OUTPUTS + j * BANK
                 nc.tensor.matmul_mx(
-                    out=ps[:], lhsT=z_codes[i][:, c].bitcast(FP8X4), lhsT_scale=z_planes[i][:, c],
-                    rhs=wo[:, 2 * n:2 * (n + NB)].bitcast(FP4X4), rhs_scale=wo_sc[:, n:n + NB],
-                    start=(g == 0), stop=(g == G - 1))
-            return ps
-
-        def finish(i, j, ps, helped):
-            c = slice(j * NB, (j + 1) * NB)
-            o = o_tiles[i]
-            if helped:
-                nc.scalar.copy(out=o[:, c], in_=ps[:])
-                nc.gpsimd.tensor_tensor(out=o[:, c], in0=o[:, c], in1=b_all[:, c], op=ADD)
+                    out=sums[:],
+                    lhsT=z_codes[i][:, tokens].bitcast(FP8X4),
+                    lhsT_scale=z_scale_bytes[i][:, tokens],
+                    rhs=w_out_codes[:, n * CODE:(n + BANK) * CODE].bitcast(FP4X4),
+                    rhs_scale=w_out_scale_bytes[:, n:n + BANK],
+                    start=(g == 0),
+                    stop=(g == PASSES - 1),
+                )
+            columns = slice(j * BANK, (j + 1) * BANK)
+            rows = out_rows[i][:, columns]
+            if s in SHARED_BLOCKS:
+                nc.scalar.copy(out=rows, in_=sums[:])
+                nc.gpsimd.tensor_tensor(out=rows, in0=rows, in1=b_out_all[:, columns], op=ADD)
             else:
-                nc.vector.tensor_tensor(out=o[:, c], in0=ps[:], in1=b_all[:, c], op=ADD)
-            width = 1 if i == TILES - 1 and j >= 6 else 2
-            if (j + 1) % width == 0:
-                c = slice((j + 1 - width) * NB, (j + 1) * NB)
-                nc.sync.dma_start(out=out[i * TOK:(i + 1) * TOK, c], in_=o[:, c])
+                nc.vector.tensor_tensor(out=rows, in0=sums[:], in1=b_out_all[:, columns], op=ADD)
+            blocks = 1 if i == TILES - 1 else 2
+            if (j + 1) % blocks == 0:
+                columns = slice((j + 1 - blocks) * BANK, (j + 1) * BANK)
+                nc.sync.dma_start(out=out[i * TILE:(i + 1) * TILE, columns], in_=out_rows[i][:, columns])
 
-        hold = {}
-        plan = []
+        permute_codes(SECOND, 1)
+        warm_up()
+        spread3 = spread_b_out(3)
+        permute_codes(SECOND, 0)
+        widen_y(0, 1)
+        copy_b_out(3, spread3)
+        y_turned = turn_y(0, 1)
+        permute_scales(SECOND, 0)
+        widen_y(1, 1)
+        spread0 = spread_b_out(0)
+        spread2 = spread_b_out(2)
+        permute_scales(SECOND, 1)
+        scale_y(0, 1, y_turned)
+        permute_codes(INTER, 0)
+        permute_codes(INTER, 1)
+        quantize_y(0, 1)
+        turn_biases()
+        y_turned = turn_y(1, 1)
+        widen_y(2, 2)
+        scale_y(1, 1, y_turned)
+        second = [branch(0, SECOND, g) for g in range(PASSES)]
+        permute_scales(INTER, 1)
+        first_turned = turn_first(0)
+        inter1 = branch(0, INTER, 1)
+        permute_scales(INTER, 0)
+        product = [gate(g, second[g], first_turned) for g in range(PASSES)]
+        inter0 = branch(0, INTER, 0)
+        quantize_y(1, 1)
+        copy_b_out(0, spread0)
+        copy_b_out(2, spread2)
+        fuse(nc.vector, 0, 1, product[1], inter1)
+        fuse(nc.vector, 0, 0, product[0], inter0)
+        quantize_z(0)
+        y_turned = turn_y(2, 2)
+        scale_y(2, 2, y_turned)
+        spread1 = spread_b_out(1)
 
-        def ev(name):
-            if name[:5] == "widen":
-                n = int(name[5:])
-                widen(n)
-            elif name[:5] == "turny":
-                hold[name] = turn_y(int(name[5:]))
-            elif name[:6] == "scaley":
-                n = name[6:]
-                (scale_y if YS[int(n)] == "v" else scale_y_s)(int(n), hold["turny" + n])
-            elif name[:6] == "quanty":
-                quantize_y(int(name[6:]))
-            elif name[:5] == "pcode":
-                permute_codes(int(name[5]), int(name[6]))
-            elif name[:6] == "pscale":
-                permute_scales(int(name[6]), int(name[7]))
-            elif name == "tbias":
-                turn_bias()
-            elif name[:6] == "spread":
-                hold[name] = spread_bias(int(name[6:]))
-            elif name[:5] == "bcopy":
-                copy_bias(int(name[5:]), hold["spread" + name[5:]])
-            elif name[:5] == "turnf":
-                hold[name] = turn_first(int(name[5:]))
-            elif name[:4] == "gate":
-                g, n = name[4], name[5]
-                hold["q" + g + n] = gate(int(g), hold["a" + g + n], hold["turnf" + n])
-            elif name[:4] == "fuse":
-                g, n = name[4], name[5]
-                fuse(nc.gpsimd if GF[int(n)][int(g)] == "g" else nc.vector, int(n), int(g), hold["q" + g + n], hold["c" + g + n])
-            elif name[:6] == "quantz":
-                quantize_z(int(name[6:]))
-            elif name[0] in "ac":
-                w = 0 if name[0] == "a" else 1
-                g, n = name[1], name[2]
-                hold[name] = relu(w, int(g), multiply(int(n), w, int(g)))
+        stage = {}
 
-        for k, name in enumerate(HEAD):
-            plan.append((k - 100.0, name))
-        for name, key in LATE.items():
-            plan.append((key, name))
-        for n in range(1, TILES):
-            for name, key in SLOT.items():
-                plan.append((key + BANKS * (n - 1), name + str(n)))
-        for s in range(TILES * BANKS):
-            plan.append((float(s), s))
-        for key, name in sorted(plan, key=lambda x: x[0]):
-            if isinstance(name, int):
-                i, j = divmod(name, BANKS)
-                finish(i, j, head(i, j), helped=(name in HELP))
-            else:
-                ev(name)
+        def step(r, i):
+            if r == -5:
+                stage[i, "second"] = [branch(i, SECOND, g) for g in range(PASSES)]
+            elif r == -1:
+                first_turned = turn_first(i)
+                stage[i, "product"] = [gate(g, stage[i, "second"][g], first_turned) for g in range(PASSES)]
+            elif r == 0:
+                stage[i, "inter"] = [branch(i, INTER, 0)]
+            elif r == 3:
+                stage[i, "inter"].append(branch(i, INTER, 1))
+            elif r in (5, 6):
+                g = r - 5
+                fuse(nc.gpsimd, i, g, stage[i, "product"][g], stage[i, "inter"][g])
+            elif r == 7:
+                quantize_z(i)
+
+        step(-5, 1)
+        step(-1, 1)
+        quantize_y(2, 2)
+        for s in range(TILES * BLOCKS):
+            if s == 2:
+                copy_b_out(1, spread1)
+            for i in range(1, TILES):
+                step(s - BLOCKS * (i - 1), i)
+            output_block(s)

from contextlib import ExitStack

import concourse.mybir as mybir
from concourse.masks import make_identity

F32 = mybir.dt.float32
BF16 = mybir.dt.bfloat16
I32 = mybir.dt.int32
U32 = mybir.dt.uint32
U8 = mybir.dt.uint8
FP8 = mybir.dt.float8_e4m3fn
FP8X4 = mybir.dt.float8_e4m3fn_x4
FP4X4 = mybir.dt.float4_e2m1fn_x4
ADD = mybir.AluOpType.add
MULT = mybir.AluOpType.mult
RELU = mybir.ActivationFunctionType.Relu

TOKENS, FEATURES, CHANNELS, OUTPUTS = 512, 512, 1024, 4096

P = 128
PACK = 4
K_PASS = P * PACK
PASSES = CHANNELS // K_PASS
TILE = 128
TILES = TOKENS // TILE
BANK = 512
BLOCKS = OUTPUTS // BANK
CODE = 2
SCALE_ROWS = 4
SECOND, INTER = 0, 1

SHARED_BLOCKS = (6, 14)
WARM_UP_MATMULS = 5

FLOPS = 2 * TOKENS * FEATURES * CHANNELS * 2 + 2 * TOKENS * CHANNELS * OUTPUTS


def tile_smcrossbaby_1_pb_w4_kernel(
    tc, y2_bytes, y2_scale, first, w_second_words, w_second_scales, b_second, w_int_words, w_int_scales, b_int,
    w_out_words, w_out_scales, b_out, out,
):
    nc = tc.nc

    with ExitStack() as ctx:
        keep = ctx.enter_context(tc.tile_pool(name="keep", bufs=1))
        work = ctx.enter_context(tc.tile_pool(name="work", bufs=4))
        psum = ctx.enter_context(tc.psum_pool(name="psum", bufs=1))
        ctx.enter_context(tc.manual_schedule())

        def kept(name, width, dtype):
            return keep.tile([P, width], dtype, name=name, align_bytes=64)

        def bank(name, width, dtype):
            return psum.tile([P, width], dtype, name=name, tag="bank", bufs=4)

        identity = kept("identity", P, F32)
        identity_bf16 = kept("identity_bf16", P, BF16)
        zeros = kept("zeros", BANK, BF16)
        table_probe = kept("table_probe", 2, F32)
        y_bytes = kept("y_bytes", TILES * FEATURES, U8)
        y_values = kept("y_values", TILES * FEATURES, BF16)
        y_scale = kept("y_scale", PACK, F32)
        y_packed = kept("y_packed", TOKENS * PACK, BF16)
        y_codes = kept("y_codes", TOKENS, U32)
        y_scale_bytes = kept("y_scale_bytes", TOKENS, U8)
        w_codes = [kept(f"w_codes{w}", CHANNELS * CODE, U8) for w in (SECOND, INTER)]
        w_scale_bytes = [kept(f"w_scale_bytes{w}", CHANNELS, U8) for w in (SECOND, INTER)]
        w_codes_by_t = [kept(f"w_codes_by_t{w}", CHANNELS * CODE, U8) for w in (SECOND, INTER)]
        w_scale_bytes_by_t = [kept(f"w_scale_bytes_by_t{w}", CHANNELS, U8) for w in (SECOND, INTER)]
        bias_rows = kept("bias_rows", K_PASS, BF16)
        bias = kept("bias", PACK * 2 * PASSES, F32)
        first_rows = [kept(f"first_rows{i}", CHANNELS, BF16) for i in range(TILES)]
        z_packed = [kept(f"z_packed{i}", PASSES * TILE * PACK, BF16) for i in range(TILES)]
        z_codes = [kept(f"z_codes{i}", PASSES * TILE, U32) for i in range(TILES)]
        z_scale_bytes = [kept(f"z_scale_bytes{i}", PASSES * TILE, U8) for i in range(TILES)]
        w_out_codes = kept("w_out_codes", PASSES * OUTPUTS * CODE, U8)
        w_out_scale_bytes = kept("w_out_scale_bytes", PASSES * OUTPUTS, U8)
        b_out_rows = kept("b_out_rows", BANK, BF16)
        b_out_all = kept("b_out_all", OUTPUTS, BF16)
        out_rows = [kept(f"out_rows{i}", OUTPUTS, F32) for i in range(TILES)]

        nc.vector.memset(b_out_rows[:], 0.0)
        nc.vector.memset(zeros[:], 0.0)
        nc.vector.memset(w_scale_bytes[SECOND][:].bitcast(I32), 0)
        nc.vector.memset(table_probe[:], 0.0)
        nc.vector.memset(bias_rows[:], 0.0)
        nc.vector.memset(w_scale_bytes[INTER][:].bitcast(I32), 0)
        nc.vector.memset(w_out_scale_bytes[:].bitcast(I32), 0)
        nc.scalar.dma_start(out=b_out_rows[0:BLOCKS, :], in_=b_out.rearrange("(j n) -> j n", j=BLOCKS))
        nc.scalar.activation(out=table_probe[:, 1:2], in_=table_probe[:, 0:1], func=RELU)

        words = (w_second_words, w_int_words)
        scales = (w_second_scales, w_int_scales)

        def load_words(w):
            nc.sync.dma_start(out=w_codes[w][:].bitcast(I32), in_=words[w][0].bitcast(I32))

        def load_scales(w):
            for r in range(SCALE_ROWS):
                nc.sync.dma_start(
                    out=w_scale_bytes[w][r:P:32, :].bitcast(I32), in_=scales[w][0][r:16:SCALE_ROWS, :].bitcast(I32)
                )

        def load_first(i):
            nc.sync.dma_start(out=first_rows[i][:], in_=first[i * TILE:(i + 1) * TILE, :])

        nc.gpsimd.dma_start(out=y_scale[:], in_=y2_scale.rearrange("o (p t) -> p (o t)", t=PACK))
        make_identity(nc, identity[:])
        load_words(SECOND)
        nc.sync.dma_start(out=y_bytes[:, 0:FEATURES], in_=y2_bytes[0:P, :])
        load_scales(SECOND)
        for w, b in enumerate((b_second, b_int)):
            nc.sync.dma_start(
                out=bias_rows[PASSES * w:PASSES * (w + 1), :], in_=b.rearrange("(g n) -> g n", g=PASSES)
            )
        load_words(INTER)
        nc.sync.dma_start(
            out=y_bytes[:, FEATURES:].rearrange("p (i k) -> p i k", k=FEATURES),
            in_=y2_bytes.rearrange("(i p) k -> p i k", p=P)[:, 1:, :],
        )
        load_scales(INTER)
        load_first(0)
        load_first(1)
        w_out_scale_rows = w_out_scales.bitcast(I32).rearrange("g (q r) n -> r q g n", r=SCALE_ROWS)
        for r in range(SCALE_ROWS):
            nc.sync.dma_start(
                out=w_out_scale_bytes[r:P:32, :].bitcast(I32).rearrange("p (g n) -> p g n", g=PASSES),
                in_=w_out_scale_rows[r],
            )
        w_out_source = w_out_words.bitcast(I32).rearrange("g p n -> p g n")
        w_out_target = w_out_codes[:].bitcast(I32).rearrange("p (g n) -> p g n", g=PASSES)
        quarter = OUTPUTS * CODE // 4 // 4
        for c in range(4):
            if c >= 2:
                load_first(c)
            columns = slice(c * quarter, (c + 1) * quarter)
            nc.sync.dma_start(out=w_out_target[:, :, columns], in_=w_out_source[:, :, columns])

        nc.scalar.copy(out=identity_bf16[:], in_=identity[:])

        def turn_biases():
            turned = bank("biases_turned", PACK * P, BF16)
            for t in range(PACK):
                nc.tensor.transpose(turned[:, t * P:(t + 1) * P], bias_rows[:, t:K_PASS:PACK], identity_bf16[:])
            nc.scalar.copy(
                out=bias[:].rearrange("p (t x) -> p t x", t=PACK),
                in_=turned[:].rearrange("p (t x) -> p t x", t=PACK)[:, :, 0:2 * PASSES],
            )

        def spread_b_out(c):
            spread = bank("b_out_spread", 2 * BANK, BF16)
            for e in range(2):
                j = 2 * c + e
                nc.tensor.matmul(
                    spread[:, e * BANK:(e + 1) * BANK],
                    lhsT=identity_bf16[:, j:j + 1].to_broadcast([P, P]),
                    rhs=b_out_rows[:],
                    start=True,
                    stop=True,
                )
            return spread

        def copy_b_out(c, spread):
            nc.scalar.copy(out=b_out_all[:, c * 2 * BANK:(c + 1) * 2 * BANK], in_=spread[:])

        def warm_up():
            sums = psum.tile([P, BANK], F32, name="branch_sums", tag="branch_sums", bufs=3)
            for k in range(WARM_UP_MATMULS):
                nc.tensor.matmul(sums[:], lhsT=zeros[:, 0:P], rhs=zeros[:], start=True, stop=True)

        def widen_y(i, n):
            columns = slice(i * FEATURES, (i + n) * FEATURES)
            nc.scalar.copy(out=y_values[:, columns], in_=y_bytes[:, columns].bitcast(FP8))

        def turn_y(i, n):
            turned = bank("y_turned", 2 * n * TILE, F32)
            for k in range(n):
                pairs = y_values[:, (i + k) * FEATURES:(i + k + 1) * FEATURES].bitcast(F32)
                for u in range(2):
                    c = (u * n + k) * TILE
                    nc.tensor.transpose(turned[:, c:c + TILE], pairs[:, u:2 * P:2], identity[:])
            return turned

        def scale_y(i, n, turned):
            nc.vector.tensor_tensor(
                out=y_packed[:, i * TILE * PACK:(i + n) * TILE * PACK].rearrange("p (r u e) -> p r u e", u=2, e=2),
                in0=turned[:].bitcast(BF16).rearrange("p (u r e) -> p r u e", u=2, e=2),
                in1=y_scale[:].rearrange("p (u e) -> p u e", e=2).unsqueeze(1).to_broadcast([P, n * TILE, 2, 2]),
                op=MULT,
            )

        def quantize_y(i, n):
            tokens = slice(i * TILE, (i + n) * TILE)
            nc.vector.quantize_mx(
                out=y_codes[:, tokens].bitcast(FP8X4),
                scales=y_scale_bytes[:, tokens],
                in_=y_packed[:, i * TILE * PACK:(i + n) * TILE * PACK],
            )

        def permute_codes(w, g):
            columns = slice(g * K_PASS * CODE, (g + 1) * K_PASS * CODE)
            nc.vector.tensor_copy(
                out=w_codes_by_t[w][:, columns].rearrange("p (t m b) -> p t m b", t=PACK, b=CODE),
                in_=w_codes[w][:, columns].rearrange("p (m t b) -> p t m b", t=PACK, b=CODE),
            )

        def permute_scales(w, g):
            columns = slice(g * K_PASS, (g + 1) * K_PASS)
            nc.vector.tensor_copy(
                out=w_scale_bytes_by_t[w][:, columns].rearrange("p (t m) -> p t m", t=PACK),
                in_=w_scale_bytes[w][:, columns].rearrange("p (m t) -> p t m", t=PACK),
            )

        def branch(i, w, g):
            sums = psum.tile([P, PACK * TILE], F32, name="branch_sums", tag="branch_sums", bufs=3)
            tokens = slice(i * TILE, (i + 1) * TILE)
            for t in range(PACK):
                n = g * PACK + t
                nc.tensor.matmul_mx(
                    out=sums[:, t * TILE:(t + 1) * TILE],
                    lhsT=w_codes_by_t[w][:, n * P * CODE:(n + 1) * P * CODE].bitcast(FP4X4),
                    lhsT_scale=w_scale_bytes_by_t[w][:, n * P:(n + 1) * P],
                    rhs=y_codes[:, tokens].bitcast(FP8X4),
                    rhs_scale=y_scale_bytes[:, tokens],
                    start=True,
                    stop=True,
                )
            result = work.tile([P, PACK * TILE], F32, name=f"branch{w}", tag=f"branch{w}", bufs=4)
            for t in range(PACK):
                columns = slice(t * TILE, (t + 1) * TILE)
                b = (t * 2 + w) * PASSES + g
                nc.scalar.activation(out=result[:, columns], in_=sums[:, columns], func=RELU, bias=bias[:, b:b + 1])
            return result

        def turn_first(i):
            turned = psum.tile([P, BANK], F32, name="first_turned", tag="first_turned", bufs=1)
            pairs = first_rows[i][:].bitcast(F32)
            for g in range(PASSES):
                for u in range(2):
                    c = (2 * g + u) * TILE
                    nc.tensor.transpose(
                        turned[:, c:c + TILE], pairs[:, 2 * P * g + u:2 * P * (g + 1):2], identity[:]
                    )
            return turned

        def gate(g, second, first_turned):
            product = work.tile([P, PACK * TILE], F32, name="product", tag="product", bufs=4)
            pairs = first_turned[:, g * 2 * TILE:(g + 1) * 2 * TILE].bitcast(BF16)
            nc.vector.tensor_tensor(
                out=product[:].rearrange("p (u e r) -> p u e r", u=2, e=2),
                in0=second[:].rearrange("p (u e r) -> p u e r", u=2, e=2),
                in1=pairs.rearrange("p (u r e) -> p u e r", u=2, e=2),
                op=MULT,
            )
            return product

        def fuse(engine, i, g, product, inter):
            engine.tensor_tensor(
                out=z_packed[i][:, g * TILE * PACK:(g + 1) * TILE * PACK].rearrange(
                    "p (c r t) -> p c t r", r=4, t=PACK
                ),
                in0=product[:].rearrange("p (t c r) -> p c t r", t=PACK, r=4),
                in1=inter[:].rearrange("p (t c r) -> p c t r", t=PACK, r=4),
                op=ADD,
            )

        def quantize_z(i):
            nc.vector.quantize_mx(
                out=z_codes[i][:].bitcast(FP8X4), scales=z_scale_bytes[i][:], in_=z_packed[i][:]
            )

        def output_block(s):
            i, j = divmod(s, BLOCKS)
            sums = bank("out_sums", BANK, F32)
            for g in range(PASSES):
                tokens = slice(g * TILE, (g + 1) * TILE)
                n = g * OUTPUTS + j * BANK
                nc.tensor.matmul_mx(
                    out=sums[:],
                    lhsT=z_codes[i][:, tokens].bitcast(FP8X4),
                    lhsT_scale=z_scale_bytes[i][:, tokens],
                    rhs=w_out_codes[:, n * CODE:(n + BANK) * CODE].bitcast(FP4X4),
                    rhs_scale=w_out_scale_bytes[:, n:n + BANK],
                    start=(g == 0),
                    stop=(g == PASSES - 1),
                )
            columns = slice(j * BANK, (j + 1) * BANK)
            rows = out_rows[i][:, columns]
            if s in SHARED_BLOCKS:
                nc.scalar.copy(out=rows, in_=sums[:])
                nc.gpsimd.tensor_tensor(out=rows, in0=rows, in1=b_out_all[:, columns], op=ADD)
            else:
                nc.vector.tensor_tensor(out=rows, in0=sums[:], in1=b_out_all[:, columns], op=ADD)
            blocks = 1 if i == TILES - 1 else 2
            if (j + 1) % blocks == 0:
                columns = slice((j + 1 - blocks) * BANK, (j + 1) * BANK)
                nc.sync.dma_start(out=out[i * TILE:(i + 1) * TILE, columns], in_=out_rows[i][:, columns])

        permute_codes(SECOND, 1)
        warm_up()
        spread3 = spread_b_out(3)
        permute_codes(SECOND, 0)
        widen_y(0, 1)
        copy_b_out(3, spread3)
        y_turned = turn_y(0, 1)
        permute_scales(SECOND, 0)
        widen_y(1, 1)
        spread0 = spread_b_out(0)
        spread2 = spread_b_out(2)
        permute_scales(SECOND, 1)
        scale_y(0, 1, y_turned)
        permute_codes(INTER, 0)
        permute_codes(INTER, 1)
        quantize_y(0, 1)
        turn_biases()
        y_turned = turn_y(1, 1)
        widen_y(2, 2)
        scale_y(1, 1, y_turned)
        second = [branch(0, SECOND, g) for g in range(PASSES)]
        permute_scales(INTER, 1)
        first_turned = turn_first(0)
        inter1 = branch(0, INTER, 1)
        permute_scales(INTER, 0)
        product = [gate(g, second[g], first_turned) for g in range(PASSES)]
        inter0 = branch(0, INTER, 0)
        quantize_y(1, 1)
        copy_b_out(0, spread0)
        copy_b_out(2, spread2)
        fuse(nc.vector, 0, 1, product[1], inter1)
        fuse(nc.vector, 0, 0, product[0], inter0)
        quantize_z(0)
        y_turned = turn_y(2, 2)
        scale_y(2, 2, y_turned)
        spread1 = spread_b_out(1)

        stage = {}

        def step(r, i):
            if r == -5:
                stage[i, "second"] = [branch(i, SECOND, g) for g in range(PASSES)]
            elif r == -1:
                first_turned = turn_first(i)
                stage[i, "product"] = [gate(g, stage[i, "second"][g], first_turned) for g in range(PASSES)]
            elif r == 0:
                stage[i, "inter"] = [branch(i, INTER, 0)]
            elif r == 3:
                stage[i, "inter"].append(branch(i, INTER, 1))
            elif r in (5, 6):
                g = r - 5
                fuse(nc.gpsimd, i, g, stage[i, "product"][g], stage[i, "inter"][g])
            elif r == 7:
                quantize_z(i)

        step(-5, 1)
        step(-1, 1)
        quantize_y(2, 2)
        for s in range(TILES * BLOCKS):
            if s == 2:
                copy_b_out(1, spread1)
            for i in range(1, TILES):
                step(s - BLOCKS * (i - 1), i)
            output_block(s)
